import numpy as np
import ml_dtypes


def mxq(x, axis, fmt="e4m3"):
    dtype, down = {"e4m3": (ml_dtypes.float8_e4m3fn, 7), "e5m2": (ml_dtypes.float8_e5m2, 14)}[fmt]
    v = np.moveaxis(np.asarray(x, np.float32).astype(ml_dtypes.bfloat16).astype(np.float64), axis, -1)
    blocks = v.reshape(v.shape[:-1] + (-1, 32))
    amax = np.abs(blocks).max(-1, keepdims=True)
    byte = np.maximum(np.where(amax > 0, np.frexp(amax)[1] - 1 + 127, 0) - down, 1)
    scale = np.exp2(byte - 127.0)
    codes = (blocks / scale).astype(np.float32).astype(dtype).astype(np.float64)
    return np.moveaxis((codes * scale).reshape(v.shape), -1, axis)


WIDE = False


def mx_kscale(k):
    if not WIDE:
        return np.ones(k)
    levels = np.array([10, -10, 5, -5, 0])
    a = np.random.permutation(np.resize(levels, k // 512 * 4)).reshape(k // 512, 4)
    idx = np.arange(k)
    return np.exp2(a[idx // 512, idx % 128 // 32])


BF16 = ml_dtypes.bfloat16


def bf(x):
    return np.asarray(x, np.float32).astype(BF16)


def f64(x):
    return np.asarray(x).astype(np.float64)


B, H, W, D, K = 2, 128, 128, 512, 128
N = H * W
EPS = 1e-12


def setup_inputs():
    s = mx_kscale(D)
    return {"x": bf(np.random.standard_normal((B, H, W, D)) * s),
            "Wk": bf(np.random.standard_normal((D, K)) * 1.5 / np.sqrt(D) / s[:, None]),
            "b": bf(np.random.standard_normal(K)),
            "C": bf(np.random.standard_normal((D, K)) * 2.0 / np.sqrt(N) * s[:, None])}


def reference(x, Wk, b, C):
    xf = f64(x).reshape(B, N, D)
    s = (mxq(xf, 2, "e4m3") @ mxq(f64(Wk), 0, "e4m3")) + f64(b)
    e = np.exp(s - s.max(-1, keepdims=True))
    af = e / e.sum(-1, keepdims=True)
    v = (mxq(xf, 1, "e4m3").transpose(0, 2, 1) @ mxq(af, 1, "e4m3")) + af.sum(axis=1)[:, None, :] * f64(C)[None]
    v = v / np.sqrt(np.sum(v * v, axis=1, keepdims=True) + EPS)
    flat = v.reshape(B, D * K)
    return flat / np.sqrt(np.sum(flat * flat, axis=-1, keepdims=True) + EPS)

@@ -1,0 +1,340 @@
+from contextlib import ExitStack
+
+import concourse.mybir as mybir
+from concourse.masks import make_identity
+
+F32 = mybir.dt.float32
+BF16 = mybir.dt.bfloat16
+U32 = mybir.dt.uint32
+U8 = mybir.dt.uint8
+FP8X4 = mybir.dt.float8_e4m3fn_x4
+ALU = mybir.AluOpType
+ACT = mybir.ActivationFunctionType
+AXIS = mybir.AxisListType
+
+P = 128
+PACK = 4
+IMAGES = 2
+POSITIONS = 16384
+FEATURES = 512
+CLUSTERS = 128
+EPS = 1e-12
+
+CHUNK = P * PACK
+CHUNKS_PER_IMAGE = POSITIONS // CHUNK
+CHUNKS = IMAGES * CHUNKS_PER_IMAGE
+FEATURE_TILES = FEATURES // P
+WORDS = FEATURES // 2
+
+VECTOR_FEATURES = 144
+
+LOADS_AHEAD = 7
+
+FLOPS = 2 * 2 * IMAGES * POSITIONS * FEATURES * CLUSTERS
+
+
+def tile_netvlad_k_kernel(tc, x, Wk, b, C, out):
+    nc = tc.nc
+    x_rows = x.rearrange("i h w d -> i (h w) d")
+
+    with ExitStack() as ctx:
+        const = ctx.enter_context(tc.tile_pool(name="const", bufs=1))
+        x_pool = ctx.enter_context(tc.tile_pool(name="x_pool", bufs=LOADS_AHEAD + 1))
+        work = ctx.enter_context(tc.tile_pool(name="work", bufs=3))
+        xt_psum = ctx.enter_context(tc.psum_pool(name="xt_psum", bufs=4))
+        s_psum = ctx.enter_context(tc.psum_pool(name="s_psum", bufs=2))
+        v_psum = ctx.enter_context(tc.psum_pool(name="v_psum", bufs=1))
+        sum_psum = ctx.enter_context(tc.psum_pool(name="sum_psum", bufs=1))
+        ctx.enter_context(tc.manual_schedule())
+
+        x_natural = {}
+        x_transposed = {}
+        xd_grouped = {}
+        xd_quantised = {}
+        logits_psum = {}
+        logits = {}
+        neg_max = {}
+        exps = {}
+        exp_sums = {}
+        recip_sums = {}
+        a_grouped = {}
+        a_quantised = {}
+        xn_grouped = {}
+        xn_quantised = {}
+        v_banks = {}
+
+        def load(c):
+            image, chunk_in_image = divmod(c, CHUNKS_PER_IMAGE)
+            first = chunk_in_image * CHUNK
+            x_nat = x_pool.tile([P, PACK, FEATURES], BF16)
+            nc.sync.dma_start(
+                out=x_nat[:],
+                in_=x_rows[image, first : first + CHUNK, :].rearrange("(p j) d -> p j d", j=PACK),
+            )
+            x_natural[c] = x_nat
+
+        for c in range(LOADS_AHEAD - 2):
+            load(c)
+
+        identity = const.tile([P, P], F32)
+        make_identity(nc, identity[:])
+        ones = const.tile([P, P], F32)
+        nc.vector.memset(ones[:], 1.0)
+
+        wk_raw = const.tile([P, PACK, CLUSTERS], BF16)
+        for u in range(2):
+            nc.scalar.dma_start(
+                out=wk_raw[:, 2 * u : 2 * u + 2, :],
+                in_=Wk[u * 2 * P : (u + 1) * 2 * P, :].rearrange("(q e) k -> q e k", e=2),
+            )
+        wk_grouped = const.tile([P, CLUSTERS, PACK], BF16, align_bytes=64)
+        nc.vector.tensor_copy(out=wk_grouped[:], in_=wk_raw[:].rearrange("q t k -> q k t"))
+        wk_codes = const.tile([P, CLUSTERS], U32, align_bytes=64)
+        wk_scales = const.tile([P, CLUSTERS], U8, align_bytes=64)
+
+        bias_bf16 = const.tile([P, CLUSTERS], BF16)
+        nc.scalar.dma_start(out=bias_bf16[:], in_=b.partition_broadcast(P))
+        bias = const.tile([P, CLUSTERS], F32)
+        nc.vector.tensor_copy(out=bias[:], in_=bias_bf16[:])
+
+        nc.vector.quantize_mx(
+            out=wk_codes[:].bitcast(FP8X4),
+            scales=wk_scales[:],
+            in_=wk_grouped[:].rearrange("q k t -> q (k t)"),
+        )
+
+        c_raw = const.tile([P, FEATURE_TILES, CLUSTERS], BF16)
+        nc.scalar.dma_start(out=c_raw[:], in_=C.rearrange("(f p) k -> p f k", p=P))
+        c_f32 = const.tile([P, FEATURE_TILES, CLUSTERS], F32)
+        nc.vector.tensor_copy(out=c_f32[:], in_=c_raw[:])
+        c_psum = xt_psum.tile([P, FEATURE_TILES, P], F32, tag="xt")
+        for f in range(FEATURE_TILES):
+            nc.tensor.transpose(c_psum[:, f, :], c_f32[:, f, :], identity[:])
+        c_transposed = const.tile([P, FEATURES], F32)
+        nc.vector.tensor_copy(out=c_transposed[:], in_=c_psum[:].rearrange("k f p -> k (f p)"))
+
+        a_sums_psum = sum_psum.tile([P, IMAGES], F32, tag="sums")
+        v_all = const.tile([P, IMAGES, FEATURES], F32)
+        v_sumsq = const.tile([P, IMAGES], F32)
+
+        def transpose_features(c):
+            x_words = x_natural[c][:].bitcast(F32)
+            banks = []
+            for h in range(2):
+                xt = xt_psum.tile([P, 2, 2 * P], F32, tag="xt")
+                for jj in range(2):
+                    for u in range(2):
+                        nc.tensor.transpose(
+                            xt[:, u, jj * P : (jj + 1) * P],
+                            x_words[:, 2 * h + jj, u * P : (u + 1) * P],
+                            identity[:],
+                        )
+                banks.append(xt)
+            x_transposed[c] = banks
+
+        def copy_transposed(c):
+            xd = work.tile([P, CHUNK * PACK], BF16, align_bytes=64)
+            xd_words = xd[:].bitcast(F32).rearrange("q (n u) -> q n u", u=2)
+            for h in range(2):
+                nc.scalar.copy(
+                    out=xd_words[:, h * 2 * P : (h + 1) * 2 * P, :],
+                    in_=x_transposed[c][h][:].rearrange("q u n -> q n u"),
+                )
+            xd_grouped[c] = xd
+
+        def quantise_along_features(c):
+            xd_codes = work.tile([P, CHUNK], U32, align_bytes=64)
+            xd_scales = work.tile([P, CHUNK], U8, align_bytes=64)
+            nc.vector.quantize_mx(
+                out=xd_codes[:].bitcast(FP8X4), scales=xd_scales[:], in_=xd_grouped[c][:]
+            )
+            xd_quantised[c] = (xd_codes, xd_scales)
+
+        def first_matmul(c):
+            xd_codes, xd_scales = xd_quantised[c]
+            s_bank = s_psum.tile([P, PACK, CLUSTERS], F32, tag="s")
+            for j in range(PACK):
+                nc.tensor.matmul_mx(
+                    out=s_bank[:, j, :],
+                    lhsT=xd_codes[:, j * P : (j + 1) * P].bitcast(FP8X4),
+                    lhsT_scale=xd_scales[:, j * P : (j + 1) * P],
+                    rhs=wk_codes[:].bitcast(FP8X4),
+                    rhs_scale=wk_scales[:],
+                    start=True,
+                    stop=True,
+                )
+            logits_psum[c] = s_bank
+
+        def add_bias(c):
+            s_biased = work.tile([P, PACK, CLUSTERS], F32)
+            nc.vector.tensor_tensor(
+                out=s_biased[:],
+                in0=logits_psum[c][:],
+                in1=bias[:].unsqueeze(1).to_broadcast([P, PACK, CLUSTERS]),
+                op=ALU.add,
+            )
+            logits[c] = s_biased
+
+        def row_max(c):
+            minus_max = work.tile([P, PACK], F32)
+            nc.vector.tensor_reduce(
+                out=minus_max[:], in_=logits[c][:], axis=AXIS.X, op=ALU.max, negate=True
+            )
+            neg_max[c] = minus_max
+
+        def exponentials(c):
+            e = work.tile([P, PACK, CLUSTERS], F32)
+            e_sum = work.tile([P, PACK], F32)
+            for j in range(PACK):
+                nc.scalar.activation(
+                    out=e[:, j, :],
+                    in_=logits[c][:, j, :],
+                    func=ACT.Exp,
+                    bias=neg_max[c][:, j : j + 1],
+                    scale=1.0,
+                    accum_out=e_sum[:, j : j + 1],
+                )
+            exps[c] = e
+            exp_sums[c] = e_sum
+
+        def normalise(c):
+            e_recip = work.tile([P, PACK], F32)
+            nc.vector.reciprocal(out=e_recip[:], in_=exp_sums[c][:])
+            a_words = work.tile([P, CLUSTERS, PACK], BF16, align_bytes=64)
+            nc.vector.tensor_tensor(
+                out=a_words[:],
+                in0=exps[c][:].rearrange("p j k -> p k j"),
+                in1=e_recip[:].unsqueeze(1).to_broadcast([P, CLUSTERS, PACK]),
+                op=ALU.mult,
+            )
+            recip_sums[c] = e_recip
+            a_grouped[c] = a_words
+
+        def quantise_assignments(c):
+            a_codes = work.tile([P, CLUSTERS], U32, align_bytes=64)
+            a_scales = work.tile([P, CLUSTERS], U8, align_bytes=64)
+            nc.vector.quantize_mx(
+                out=a_codes[:].bitcast(FP8X4),
+                scales=a_scales[:],
+                in_=a_grouped[c][:].rearrange("p k j -> p (k j)"),
+            )
+            a_quantised[c] = (a_codes, a_scales)
+
+        def group_positions(c):
+            xn = work.tile([P, FEATURES, PACK], BF16, align_bytes=64)
+            x_nat = x_natural[c]
+            nc.vector.tensor_copy(
+                out=xn[:, :VECTOR_FEATURES, :].rearrange("p (g i) j -> p g j i", i=4),
+                in_=x_nat[:, :, :VECTOR_FEATURES].rearrange("p j (g i) -> p g j i", i=4),
+            )
+            nc.scalar.copy(
+                out=xn[:, VECTOR_FEATURES:, :].rearrange("p (g i) j -> p g j i", i=4),
+                in_=x_nat[:, :, VECTOR_FEATURES:].rearrange("p j (g i) -> p g j i", i=4),
+            )
+            xn_grouped[c] = xn
+
+        def quantise_along_positions(c):
+            xn_codes = work.tile([P, FEATURES], U32, align_bytes=64)
+            xn_scales = work.tile([P, FEATURES], U8, align_bytes=64)
+            nc.vector.quantize_mx(
+                out=xn_codes[:].bitcast(FP8X4),
+                scales=xn_scales[:],
+                in_=xn_grouped[c][:].rearrange("p d j -> p (d j)"),
+            )
+            xn_quantised[c] = (xn_codes, xn_scales)
+
+        def second_matmul(c):
+            image, chunk_in_image = divmod(c, CHUNKS_PER_IMAGE)
+            first = chunk_in_image == 0
+            last = chunk_in_image == CHUNKS_PER_IMAGE - 1
+            for j in range(PACK):
+                nc.tensor.matmul(
+                    out=a_sums_psum[:, image : image + 1],
+                    lhsT=exps[c][:, j, :],
+                    rhs=recip_sums[c][:, j : j + 1],
+                    start=first and j == 0,
+                    stop=last and j == PACK - 1,
+                )
+            if first:
+                v_bank = v_psum.tile([P, FEATURES], F32, tag="v")
+                v_banks[image] = v_bank
+            a_codes, a_scales = a_quantised[c]
+            xn_codes, xn_scales = xn_quantised[c]
+            nc.tensor.matmul_mx(
+                out=v_banks[image][:],
+                lhsT=a_codes[:].bitcast(FP8X4),
+                lhsT_scale=a_scales[:],
+                rhs=xn_codes[:].bitcast(FP8X4),
+                rhs_scale=xn_scales[:],
+                start=first,
+                stop=last,
+            )
+            if last:
+                finish_image(image)
+
+        def finish_image(image):
+            a_sum = work.tile([P, 1], F32)
+            nc.vector.tensor_copy(out=a_sum[:], in_=a_sums_psum[:, image : image + 1])
+            nc.vector.scalar_tensor_tensor(
+                out=v_all[:, image, :],
+                in0=c_transposed[:],
+                scalar=a_sum[:, 0:1],
+                in1=v_banks[image][:],
+                op0=ALU.mult,
+                op1=ALU.add,
+            )
+            squares = work.tile([P, FEATURES], F32)
+            nc.scalar.activation(
+                out=squares[:],
+                in_=v_all[:, image, :],
+                func=ACT.Square,
+                accum_out=v_sumsq[:, image : image + 1],
+            )
+
+        def run(stage, c):
+            if 0 <= c < CHUNKS:
+                stage(c)
+
+        for step in range(-2, CHUNKS + 1):
+            run(load, step + LOADS_AHEAD)
+            run(transpose_features, step + 2)
+            run(add_bias, step)
+            run(quantise_assignments, step - 1)
+            run(row_max, step)
+            run(group_positions, step + 1)
+            run(second_matmul, step - 1)
+            run(exponentials, step)
+            run(quantise_along_features, step + 1)
+            run(first_matmul, step + 1)
+            run(quantise_along_positions, step)
+            run(copy_transposed, step + 2)
+            run(normalise, step)
+
+        cluster_inv = const.tile([P, IMAGES], F32)
+        nc.vector.tensor_scalar_add(out=cluster_inv[:], in0=v_sumsq[:], scalar1=EPS)
+        nc.vector.reciprocal(out=cluster_inv[:], in_=cluster_inv[:])
+        cluster_unit = const.tile([P, IMAGES], F32)
+        nc.vector.tensor_tensor(out=cluster_unit[:], in0=v_sumsq[:], in1=cluster_inv[:], op=ALU.mult)
+        total_psum = s_psum.tile([P, IMAGES], F32, tag="s")
+        nc.tensor.matmul(out=total_psum[:], lhsT=ones[:], rhs=cluster_unit[:], start=True, stop=True)
+        image_inv = const.tile([P, IMAGES], F32)
+        nc.vector.tensor_scalar_add(out=image_inv[:], in0=total_psum[:], scalar1=EPS)
+        nc.vector.reciprocal(out=image_inv[:], in_=image_inv[:])
+        factor = const.tile([P, IMAGES], F32)
+        nc.vector.tensor_tensor(out=factor[:], in0=cluster_inv[:], in1=image_inv[:], op=ALU.mult)
+        nc.scalar.sqrt(out=factor[:], in_=factor[:])
+
+        for image in range(IMAGES):
+            v_scaled = work.tile([P, FEATURES], F32)
+            nc.vector.tensor_scalar_mul(
+                out=v_scaled[:], in0=v_all[:, image, :], scalar1=factor[:, image : image + 1]
+            )
+            out_psum = xt_psum.tile([P, FEATURE_TILES, CLUSTERS], F32, tag="xt")
+            for f in range(FEATURE_TILES):
+                nc.tensor.transpose(out_psum[:, f, :], v_scaled[:, f * P : (f + 1) * P], identity[:])
+            out_rows = work.tile([P, FEATURE_TILES, CLUSTERS], F32)
+            nc.scalar.copy(out=out_rows[:], in_=out_psum[:])
+            nc.sync.dma_start(
+                out=out[image, :].rearrange("(f p k) -> p f k", f=FEATURE_TILES, p=P),
+                in_=out_rows[:],
+            )

@@ -28,7 +28,20 @@ WORDS = FEATURES // 2
 
 VECTOR_FEATURES = 144
 
-LOADS_AHEAD = 7
+AT_LOAD = 10
+AT_TRANSPOSE = 6
+AT_COPY_TRANSPOSED = 5
+AT_QUANTISE_FEATURES = 4
+AT_FIRST_MATMUL = 3
+AT_BIAS_AND_MAX = 2
+AT_EXP = 1
+AT_GROUP_POSITIONS = 1
+AT_NORMALISE = 0
+AT_QUANTISE_POSITIONS = 0
+AT_QUANTISE_ASSIGNMENTS = -1
+AT_SECOND_MATMUL = -2
+FIRST_STEP = -AT_TRANSPOSE
+LAST_STEP = CHUNKS - 1 - AT_SECOND_MATMUL
 
 FLOPS = 2 * 2 * IMAGES * POSITIONS * FEATURES * CLUSTERS
 
@@ -39,8 +52,9 @@ def tile_netvlad_k_kernel(tc, x, Wk, b, C, out):
 
     with ExitStack() as ctx:
         const = ctx.enter_context(tc.tile_pool(name="const", bufs=1))
-        x_pool = ctx.enter_context(tc.tile_pool(name="x_pool", bufs=LOADS_AHEAD + 1))
+        x_pool = ctx.enter_context(tc.tile_pool(name="x_pool", bufs=AT_LOAD - AT_GROUP_POSITIONS + 2))
         work = ctx.enter_context(tc.tile_pool(name="work", bufs=3))
+        held = ctx.enter_context(tc.tile_pool(name="held", bufs=5))
         xt_psum = ctx.enter_context(tc.psum_pool(name="xt_psum", bufs=4))
         s_psum = ctx.enter_context(tc.psum_pool(name="s_psum", bufs=2))
         v_psum = ctx.enter_context(tc.psum_pool(name="v_psum", bufs=1))
@@ -73,7 +87,7 @@ def tile_netvlad_k_kernel(tc, x, Wk, b, C, out):
             )
             x_natural[c] = x_nat
 
-        for c in range(LOADS_AHEAD - 2):
+        for c in range(FIRST_STEP + AT_LOAD):
             load(c)
 
         identity = const.tile([P, P], F32)
@@ -105,13 +119,15 @@ def tile_netvlad_k_kernel(tc, x, Wk, b, C, out):
 
         c_raw = const.tile([P, FEATURE_TILES, CLUSTERS], BF16)
         nc.scalar.dma_start(out=c_raw[:], in_=C.rearrange("(f p) k -> p f k", p=P))
-        c_f32 = const.tile([P, FEATURE_TILES, CLUSTERS], F32)
-        nc.vector.tensor_copy(out=c_f32[:], in_=c_raw[:])
-        c_psum = xt_psum.tile([P, FEATURE_TILES, P], F32, tag="xt")
-        for f in range(FEATURE_TILES):
-            nc.tensor.transpose(c_psum[:, f, :], c_f32[:, f, :], identity[:])
         c_transposed = const.tile([P, FEATURES], F32)
-        nc.vector.tensor_copy(out=c_transposed[:], in_=c_psum[:].rearrange("k f p -> k (f p)"))
+
+        def transpose_centres():
+            c_f32 = const.tile([P, FEATURE_TILES, CLUSTERS], F32)
+            nc.vector.tensor_copy(out=c_f32[:], in_=c_raw[:])
+            c_psum = s_psum.tile([P, FEATURE_TILES, P], F32, tag="s")
+            for f in range(FEATURE_TILES):
+                nc.tensor.transpose(c_psum[:, f, :], c_f32[:, f, :], identity[:])
+            nc.vector.tensor_copy(out=c_transposed[:], in_=c_psum[:].rearrange("k f p -> k (f p)"))
 
         a_sums_psum = sum_psum.tile([P, IMAGES], F32, tag="sums")
         v_all = const.tile([P, IMAGES, FEATURES], F32)
@@ -183,7 +199,7 @@ def tile_netvlad_k_kernel(tc, x, Wk, b, C, out):
             neg_max[c] = minus_max
 
         def exponentials(c):
-            e = work.tile([P, PACK, CLUSTERS], F32)
+            e = held.tile([P, PACK, CLUSTERS], F32)
             e_sum = work.tile([P, PACK], F32)
             for j in range(PACK):
                 nc.scalar.activation(
@@ -197,17 +213,19 @@ def tile_netvlad_k_kernel(tc, x, Wk, b, C, out):
             exps[c] = e
             exp_sums[c] = e_sum
 
-        def normalise(c):
-            e_recip = work.tile([P, PACK], F32)
+        def invert_sums(c):
+            e_recip = held.tile([P, PACK], F32)
             nc.vector.reciprocal(out=e_recip[:], in_=exp_sums[c][:])
+            recip_sums[c] = e_recip
+
+        def normalise(c):
             a_words = work.tile([P, CLUSTERS, PACK], BF16, align_bytes=64)
             nc.vector.tensor_tensor(
                 out=a_words[:],
                 in0=exps[c][:].rearrange("p j k -> p k j"),
-                in1=e_recip[:].unsqueeze(1).to_broadcast([P, CLUSTERS, PACK]),
+                in1=recip_sums[c][:].unsqueeze(1).to_broadcast([P, CLUSTERS, PACK]),
                 op=ALU.mult,
             )
-            recip_sums[c] = e_recip
             a_grouped[c] = a_words
 
         def quantise_assignments(c):
@@ -234,8 +252,8 @@ def tile_netvlad_k_kernel(tc, x, Wk, b, C, out):
             xn_grouped[c] = xn
 
         def quantise_along_positions(c):
-            xn_codes = work.tile([P, FEATURES], U32, align_bytes=64)
-            xn_scales = work.tile([P, FEATURES], U8, align_bytes=64)
+            xn_codes = held.tile([P, FEATURES], U32, align_bytes=64)
+            xn_scales = held.tile([P, FEATURES], U8, align_bytes=64)
             nc.vector.quantize_mx(
                 out=xn_codes[:].bitcast(FP8X4),
                 scales=xn_scales[:],
@@ -295,20 +313,27 @@ def tile_netvlad_k_kernel(tc, x, Wk, b, C, out):
             if 0 <= c < CHUNKS:
                 stage(c)
 
-        for step in range(-2, CHUNKS + 1):
-            run(load, step + LOADS_AHEAD)
-            run(transpose_features, step + 2)
-            run(add_bias, step)
-            run(quantise_assignments, step - 1)
-            run(row_max, step)
-            run(group_positions, step + 1)
-            run(second_matmul, step - 1)
-            run(exponentials, step)
-            run(quantise_along_features, step + 1)
-            run(first_matmul, step + 1)
-            run(quantise_along_positions, step)
-            run(copy_transposed, step + 2)
-            run(normalise, step)
+        def pipeline_step(step):
+            run(load, step + AT_LOAD)
+            run(transpose_features, step + AT_TRANSPOSE)
+            run(second_matmul, step + AT_SECOND_MATMUL)
+            run(first_matmul, step + AT_FIRST_MATMUL)
+            run(exponentials, step + AT_EXP)
+            run(copy_transposed, step + AT_COPY_TRANSPOSED)
+            run(add_bias, step + AT_BIAS_AND_MAX)
+            run(quantise_along_features, step + AT_QUANTISE_FEATURES)
+            run(row_max, step + AT_BIAS_AND_MAX)
+            run(invert_sums, step + AT_NORMALISE)
+            run(quantise_along_positions, step + AT_QUANTISE_POSITIONS)
+            run(normalise, step + AT_NORMALISE)
+            run(group_positions, step + AT_GROUP_POSITIONS)
+            run(quantise_assignments, step + AT_QUANTISE_ASSIGNMENTS)
+
+        for step in range(FIRST_STEP, 0):
+            pipeline_step(step)
+        transpose_centres()
+        for step in range(0, LAST_STEP + 1):
+            pipeline_step(step)
 
         cluster_inv = const.tile([P, IMAGES], F32)
         nc.vector.tensor_scalar_add(out=cluster_inv[:], in0=v_sumsq[:], scalar1=EPS)

@@ -43,6 +43,8 @@ AT_SECOND_MATMUL = -2
 FIRST_STEP = -AT_TRANSPOSE
 LAST_STEP = CHUNKS - 1 - AT_SECOND_MATMUL
 
+SUM_COLUMNS = 64
+
 FLOPS = 2 * 2 * IMAGES * POSITIONS * FEATURES * CLUSTERS
 
 
@@ -129,7 +131,7 @@ def tile_netvlad_k_kernel(tc, x, Wk, b, C, out):
                 nc.tensor.transpose(c_psum[:, f, :], c_f32[:, f, :], identity[:])
             nc.vector.tensor_copy(out=c_transposed[:], in_=c_psum[:].rearrange("k f p -> k (f p)"))
 
-        a_sums_psum = sum_psum.tile([P, IMAGES], F32, tag="sums")
+        a_sums_psum = sum_psum.tile([P, IMAGES, SUM_COLUMNS], F32, tag="sums")
         v_all = const.tile([P, IMAGES, FEATURES], F32)
         v_sumsq = const.tile([P, IMAGES], F32)
 
@@ -267,9 +269,9 @@ def tile_netvlad_k_kernel(tc, x, Wk, b, C, out):
             last = chunk_in_image == CHUNKS_PER_IMAGE - 1
             for j in range(PACK):
                 nc.tensor.matmul(
-                    out=a_sums_psum[:, image : image + 1],
+                    out=a_sums_psum[:, image, :],
                     lhsT=exps[c][:, j, :],
-                    rhs=recip_sums[c][:, j : j + 1],
+                    rhs=recip_sums[c][:, j : j + 1].to_broadcast([P, SUM_COLUMNS]),
                     start=first and j == 0,
                     stop=last and j == PACK - 1,
                 )
@@ -292,7 +294,7 @@ def tile_netvlad_k_kernel(tc, x, Wk, b, C, out):
 
         def finish_image(image):
             a_sum = work.tile([P, 1], F32)
-            nc.vector.tensor_copy(out=a_sum[:], in_=a_sums_psum[:, image : image + 1])
+            nc.vector.tensor_copy(out=a_sum[:], in_=a_sums_psum[:, image, 0:1])
             nc.vector.scalar_tensor_tensor(
                 out=v_all[:, image, :],
                 in0=c_transposed[:],

@@ -223,9 +223,9 @@ def tile_netvlad_k_kernel(tc, x, Wk, b, C, out):
         def normalise(c):
             a_words = work.tile([P, CLUSTERS, PACK], BF16, align_bytes=64)
             nc.vector.tensor_tensor(
-                out=a_words[:],
-                in0=exps[c][:].rearrange("p j k -> p k j"),
-                in1=recip_sums[c][:].unsqueeze(1).to_broadcast([P, CLUSTERS, PACK]),
+                out=a_words[:].rearrange("p (g i) j -> p g j i", i=4),
+                in0=exps[c][:].rearrange("p j (g i) -> p g j i", i=4),
+                in1=recip_sums[c][:].unsqueeze(1).unsqueeze(3).to_broadcast([P, CLUSTERS // 4, PACK, 4]),
                 op=ALU.mult,
             )
             a_grouped[c] = a_words

@@ -26,18 +26,21 @@ CHUNKS = IMAGES * CHUNKS_PER_IMAGE
 FEATURE_TILES = FEATURES // P
 WORDS = FEATURES // 2
 
-VECTOR_FEATURES = 144
+POOL_FEATURES = 176
+XN_BUFS = 3
 
-AT_LOAD = 10
-AT_TRANSPOSE = 6
-AT_COPY_TRANSPOSED = 5
-AT_QUANTISE_FEATURES = 4
-AT_FIRST_MATMUL = 3
-AT_BIAS_AND_MAX = 2
+AT_LOAD = 11
+AT_TRANSPOSE = 7
+AT_COPY_TRANSPOSED = 6
+AT_QUANTISE_FEATURES = 5
+AT_FIRST_MATMUL = 4
+AT_BIAS = 3
+AT_MAX = 2
 AT_EXP = 1
 AT_GROUP_POSITIONS = 1
 AT_NORMALISE = 0
 AT_QUANTISE_POSITIONS = 0
+AT_POOL_GROUP_POSITIONS = AT_QUANTISE_POSITIONS + XN_BUFS
 AT_QUANTISE_ASSIGNMENTS = -1
 AT_SECOND_MATMUL = -2
 FIRST_STEP = -AT_TRANSPOSE
@@ -55,7 +58,8 @@ def tile_netvlad_k_kernel(tc, x, Wk, b, C, out):
     with ExitStack() as ctx:
         const = ctx.enter_context(tc.tile_pool(name="const", bufs=1))
         x_pool = ctx.enter_context(tc.tile_pool(name="x_pool", bufs=AT_LOAD - AT_GROUP_POSITIONS + 2))
-        work = ctx.enter_context(tc.tile_pool(name="work", bufs=3))
+        work = ctx.enter_context(tc.tile_pool(name="work", bufs=4))
+        xn_pool = ctx.enter_context(tc.tile_pool(name="xn_pool", bufs=XN_BUFS))
         held = ctx.enter_context(tc.tile_pool(name="held", bufs=5))
         xt_psum = ctx.enter_context(tc.psum_pool(name="xt_psum", bufs=4))
         s_psum = ctx.enter_context(tc.psum_pool(name="s_psum", bufs=2))
@@ -240,18 +244,23 @@ def tile_netvlad_k_kernel(tc, x, Wk, b, C, out):
             )
             a_quantised[c] = (a_codes, a_scales)
 
-        def group_positions(c):
-            xn = work.tile([P, FEATURES, PACK], BF16, align_bytes=64)
-            x_nat = x_natural[c]
-            nc.vector.tensor_copy(
-                out=xn[:, :VECTOR_FEATURES, :].rearrange("p (g i) j -> p g j i", i=4),
-                in_=x_nat[:, :, :VECTOR_FEATURES].rearrange("p j (g i) -> p g j i", i=4),
-            )
-            nc.scalar.copy(
-                out=xn[:, VECTOR_FEATURES:, :].rearrange("p (g i) j -> p g j i", i=4),
-                in_=x_nat[:, :, VECTOR_FEATURES:].rearrange("p j (g i) -> p g j i", i=4),
+        def pool_group_positions(c):
+            xn = xn_pool.tile([P, FEATURES, PACK], BF16, align_bytes=64)
+            nc.gpsimd.tensor_scalar(
+                out=xn[:, :POOL_FEATURES, :],
+                in0=x_natural[c][:, :, :POOL_FEATURES].rearrange("p j d -> p d j"),
+                scalar1=1.0,
+                scalar2=0.0,
+                op0=ALU.mult,
+                op1=ALU.add,
             )
             xn_grouped[c] = xn
+
+        def group_positions(c):
+            nc.scalar.copy(
+                out=xn_grouped[c][:, POOL_FEATURES:, :].rearrange("p (g i) j -> p g j i", i=4),
+                in_=x_natural[c][:, :, POOL_FEATURES:].rearrange("p j (g i) -> p g j i", i=4),
+            )
 
         def quantise_along_positions(c):
             xn_codes = held.tile([P, FEATURES], U32, align_bytes=64)
@@ -322,14 +331,15 @@ def tile_netvlad_k_kernel(tc, x, Wk, b, C, out):
             run(first_matmul, step + AT_FIRST_MATMUL)
             run(exponentials, step + AT_EXP)
             run(copy_transposed, step + AT_COPY_TRANSPOSED)
-            run(add_bias, step + AT_BIAS_AND_MAX)
-            run(quantise_along_features, step + AT_QUANTISE_FEATURES)
-            run(row_max, step + AT_BIAS_AND_MAX)
+            run(add_bias, step + AT_BIAS)
+            run(row_max, step + AT_MAX)
             run(invert_sums, step + AT_NORMALISE)
-            run(quantise_along_positions, step + AT_QUANTISE_POSITIONS)
+            run(quantise_along_features, step + AT_QUANTISE_FEATURES)
             run(normalise, step + AT_NORMALISE)
-            run(group_positions, step + AT_GROUP_POSITIONS)
             run(quantise_assignments, step + AT_QUANTISE_ASSIGNMENTS)
+            run(group_positions, step + AT_GROUP_POSITIONS)
+            run(quantise_along_positions, step + AT_QUANTISE_POSITIONS)
+            run(pool_group_positions, step + AT_POOL_GROUP_POSITIONS)
 
         for step in range(FIRST_STEP, 0):
             pipeline_step(step)

@@ -27,20 +27,20 @@ FEATURE_TILES = FEATURES // P
 WORDS = FEATURES // 2
 
 POOL_FEATURES = 176
-XN_BUFS = 3
+IN_BUFS = 3
+WIDTH = FEATURES * PACK
 
 AT_LOAD = 11
 AT_TRANSPOSE = 7
 AT_COPY_TRANSPOSED = 6
-AT_QUANTISE_FEATURES = 5
+AT_QUANTISE = 5
 AT_FIRST_MATMUL = 4
 AT_BIAS = 3
 AT_MAX = 2
 AT_EXP = 1
 AT_GROUP_POSITIONS = 1
 AT_NORMALISE = 0
-AT_QUANTISE_POSITIONS = 0
-AT_POOL_GROUP_POSITIONS = AT_QUANTISE_POSITIONS + XN_BUFS
+AT_POOL_GROUP_POSITIONS = IN_BUFS
 AT_QUANTISE_ASSIGNMENTS = -1
 AT_SECOND_MATMUL = -2
 FIRST_STEP = -AT_TRANSPOSE
@@ -59,7 +59,7 @@ def tile_netvlad_k_kernel(tc, x, Wk, b, C, out):
         const = ctx.enter_context(tc.tile_pool(name="const", bufs=1))
         x_pool = ctx.enter_context(tc.tile_pool(name="x_pool", bufs=AT_LOAD - AT_GROUP_POSITIONS + 2))
         work = ctx.enter_context(tc.tile_pool(name="work", bufs=4))
-        xn_pool = ctx.enter_context(tc.tile_pool(name="xn_pool", bufs=XN_BUFS))
+        in_pool = ctx.enter_context(tc.tile_pool(name="in_pool", bufs=IN_BUFS))
         held = ctx.enter_context(tc.tile_pool(name="held", bufs=5))
         xt_psum = ctx.enter_context(tc.psum_pool(name="xt_psum", bufs=4))
         s_psum = ctx.enter_context(tc.psum_pool(name="s_psum", bufs=2))
@@ -69,7 +69,7 @@ def tile_netvlad_k_kernel(tc, x, Wk, b, C, out):
 
         x_natural = {}
         x_transposed = {}
-        xd_grouped = {}
+        quantise_input = {}
         xd_quantised = {}
         logits_psum = {}
         logits = {}
@@ -79,7 +79,6 @@ def tile_netvlad_k_kernel(tc, x, Wk, b, C, out):
         recip_sums = {}
         a_grouped = {}
         a_quantised = {}
-        xn_grouped = {}
         xn_quantised = {}
         v_banks = {}
 
@@ -155,22 +154,34 @@ def tile_netvlad_k_kernel(tc, x, Wk, b, C, out):
             x_transposed[c] = banks
 
         def copy_transposed(c):
-            xd = work.tile([P, CHUNK * PACK], BF16, align_bytes=64)
-            xd_words = xd[:].bitcast(F32).rearrange("q (n u) -> q n u", u=2)
+            xd = quantise_input[c - AT_QUANTISE][:, :WIDTH]
+            xd_words = xd.bitcast(F32).rearrange("q (n u) -> q n u", u=2)
             for h in range(2):
                 nc.scalar.copy(
                     out=xd_words[:, h * 2 * P : (h + 1) * 2 * P, :],
                     in_=x_transposed[c][h][:].rearrange("q u n -> q n u"),
                 )
-            xd_grouped[c] = xd
 
-        def quantise_along_features(c):
-            xd_codes = work.tile([P, CHUNK], U32, align_bytes=64)
-            xd_scales = work.tile([P, CHUNK], U8, align_bytes=64)
+        def new_quantise_input(step):
+            q_in = in_pool.tile([P, 2 * WIDTH], BF16, align_bytes=64)
+            quantise_input[step] = q_in
+
+        def quantise(step):
+            along_d = 0 <= step + AT_QUANTISE < CHUNKS
+            along_n = 0 <= step < CHUNKS
+            if not along_d and not along_n:
+                return
+            first = 0 if along_d else 1
+            last = 2 if along_n else 1
+            codes = held.tile([P, 2 * CHUNK], U32, align_bytes=64)
+            scales = held.tile([P, 2 * CHUNK], U8, align_bytes=64)
             nc.vector.quantize_mx(
-                out=xd_codes[:].bitcast(FP8X4), scales=xd_scales[:], in_=xd_grouped[c][:]
+                out=codes[:, first * CHUNK : last * CHUNK].bitcast(FP8X4),
+                scales=scales[:, first * CHUNK : last * CHUNK],
+                in_=quantise_input[step][:, first * WIDTH : last * WIDTH],
             )
-            xd_quantised[c] = (xd_codes, xd_scales)
+            xd_quantised[step + AT_QUANTISE] = (codes[:, :CHUNK], scales[:, :CHUNK])
+            xn_quantised[step] = (codes[:, CHUNK:], scales[:, CHUNK:])
 
         def first_matmul(c):
             xd_codes, xd_scales = xd_quantised[c]
@@ -245,7 +256,7 @@ def tile_netvlad_k_kernel(tc, x, Wk, b, C, out):
             a_quantised[c] = (a_codes, a_scales)
 
         def pool_group_positions(c):
-            xn = xn_pool.tile([P, FEATURES, PACK], BF16, align_bytes=64)
+            xn = quantise_input[c][:, WIDTH:].rearrange("p (d j) -> p d j", j=PACK)
             nc.gpsimd.tensor_scalar(
                 out=xn[:, :POOL_FEATURES, :],
                 in0=x_natural[c][:, :, :POOL_FEATURES].rearrange("p j d -> p d j"),
@@ -254,23 +265,13 @@ def tile_netvlad_k_kernel(tc, x, Wk, b, C, out):
                 op0=ALU.mult,
                 op1=ALU.add,
             )
-            xn_grouped[c] = xn
 
         def group_positions(c):
+            xn = quantise_input[c][:, WIDTH:].rearrange("p (d j) -> p d j", j=PACK)
             nc.scalar.copy(
-                out=xn_grouped[c][:, POOL_FEATURES:, :].rearrange("p (g i) j -> p g j i", i=4),
+                out=xn[:, POOL_FEATURES:, :].rearrange("p (g i) j -> p g j i", i=4),
                 in_=x_natural[c][:, :, POOL_FEATURES:].rearrange("p j (g i) -> p g j i", i=4),
             )
-
-        def quantise_along_positions(c):
-            xn_codes = held.tile([P, FEATURES], U32, align_bytes=64)
-            xn_scales = held.tile([P, FEATURES], U8, align_bytes=64)
-            nc.vector.quantize_mx(
-                out=xn_codes[:].bitcast(FP8X4),
-                scales=xn_scales[:],
-                in_=xn_grouped[c][:].rearrange("p d j -> p (d j)"),
-            )
-            xn_quantised[c] = (xn_codes, xn_scales)
 
         def second_matmul(c):
             image, chunk_in_image = divmod(c, CHUNKS_PER_IMAGE)
@@ -293,8 +294,8 @@ def tile_netvlad_k_kernel(tc, x, Wk, b, C, out):
                 out=v_banks[image][:],
                 lhsT=a_codes[:].bitcast(FP8X4),
                 lhsT_scale=a_scales[:],
-                rhs=xn_codes[:].bitcast(FP8X4),
-                rhs_scale=xn_scales[:],
+                rhs=xn_codes.bitcast(FP8X4),
+                rhs_scale=xn_scales,
                 start=first,
                 stop=last,
             )
@@ -334,13 +335,15 @@ def tile_netvlad_k_kernel(tc, x, Wk, b, C, out):
             run(add_bias, step + AT_BIAS)
             run(row_max, step + AT_MAX)
             run(invert_sums, step + AT_NORMALISE)
-            run(quantise_along_features, step + AT_QUANTISE_FEATURES)
-            run(normalise, step + AT_NORMALISE)
             run(quantise_assignments, step + AT_QUANTISE_ASSIGNMENTS)
+            run(normalise, step + AT_NORMALISE)
             run(group_positions, step + AT_GROUP_POSITIONS)
-            run(quantise_along_positions, step + AT_QUANTISE_POSITIONS)
+            quantise(step)
+            new_quantise_input(step + IN_BUFS)
             run(pool_group_positions, step + AT_POOL_GROUP_POSITIONS)
 
+        for step in range(FIRST_STEP, FIRST_STEP + IN_BUFS):
+            new_quantise_input(step)
         for step in range(FIRST_STEP, 0):
             pipeline_step(step)
         transpose_centres()

@@ -39,12 +39,15 @@ AT_BIAS = 3
 AT_MAX = 2
 AT_EXP = 1
 AT_GROUP_POSITIONS = 1
-AT_NORMALISE = 0
+AT_INVERT_SUMS = 0
+AT_NORMALISE = -1
 AT_POOL_GROUP_POSITIONS = IN_BUFS
 AT_QUANTISE_ASSIGNMENTS = -1
 AT_SECOND_MATMUL = -2
+AT_FINISH_IMAGE = -3
 FIRST_STEP = -AT_TRANSPOSE
-LAST_STEP = CHUNKS - 1 - AT_SECOND_MATMUL
+LAST_EXP_STEP = CHUNKS - 1 - AT_EXP
+LAST_STEP = CHUNKS - 1 - AT_FINISH_IMAGE
 
 SUM_COLUMNS = 64
 
@@ -299,20 +302,23 @@ def tile_netvlad_k_kernel(tc, x, Wk, b, C, out):
                 start=first,
                 stop=last,
             )
-            if last:
-                finish_image(image)
 
-        def finish_image(image):
-            a_sum = work.tile([P, 1], F32)
-            nc.vector.tensor_copy(out=a_sum[:], in_=a_sums_psum[:, image, 0:1])
-            nc.vector.scalar_tensor_tensor(
-                out=v_all[:, image, :],
-                in0=c_transposed[:],
-                scalar=a_sum[:, 0:1],
-                in1=v_banks[image][:],
-                op0=ALU.mult,
-                op1=ALU.add,
-            )
+        def add_centres(c):
+            image, chunk_in_image = divmod(c, CHUNKS_PER_IMAGE)
+            if chunk_in_image == CHUNKS_PER_IMAGE - 1:
+                nc.vector.scalar_tensor_tensor(
+                    out=v_all[:, image, :],
+                    in0=c_transposed[:],
+                    scalar=a_sums_psum[:, image, 0:1],
+                    in1=v_banks[image][:],
+                    op0=ALU.mult,
+                    op1=ALU.add,
+                )
+
+        def sum_squares(c):
+            image, chunk_in_image = divmod(c, CHUNKS_PER_IMAGE)
+            if chunk_in_image < CHUNKS_PER_IMAGE - 1:
+                return
             squares = work.tile([P, FEATURES], F32)
             nc.scalar.activation(
                 out=squares[:],
@@ -327,6 +333,7 @@ def tile_netvlad_k_kernel(tc, x, Wk, b, C, out):
 
         def pipeline_step(step):
             run(load, step + AT_LOAD)
+            run(add_centres, step + AT_FINISH_IMAGE)
             run(transpose_features, step + AT_TRANSPOSE)
             run(second_matmul, step + AT_SECOND_MATMUL)
             run(first_matmul, step + AT_FIRST_MATMUL)
@@ -334,11 +341,12 @@ def tile_netvlad_k_kernel(tc, x, Wk, b, C, out):
             run(copy_transposed, step + AT_COPY_TRANSPOSED)
             run(add_bias, step + AT_BIAS)
             run(row_max, step + AT_MAX)
-            run(invert_sums, step + AT_NORMALISE)
-            run(quantise_assignments, step + AT_QUANTISE_ASSIGNMENTS)
+            run(invert_sums, step + AT_INVERT_SUMS)
             run(normalise, step + AT_NORMALISE)
             run(group_positions, step + AT_GROUP_POSITIONS)
+            run(sum_squares, step + AT_FINISH_IMAGE)
             quantise(step)
+            run(quantise_assignments, step + AT_QUANTISE_ASSIGNMENTS)
             new_quantise_input(step + IN_BUFS)
             run(pool_group_positions, step + AT_POOL_GROUP_POSITIONS)
 
@@ -347,7 +355,11 @@ def tile_netvlad_k_kernel(tc, x, Wk, b, C, out):
         for step in range(FIRST_STEP, 0):
             pipeline_step(step)
         transpose_centres()
-        for step in range(0, LAST_STEP + 1):
+        for step in range(0, LAST_EXP_STEP + 1):
+            pipeline_step(step)
+        unit = const.tile([P, 1], F32)
+        nc.scalar.sqrt(out=unit[:], in_=ones[:, 0:1])
+        for step in range(LAST_EXP_STEP + 1, LAST_STEP + 1):
             pipeline_step(step)
 
         cluster_inv = const.tile([P, IMAGES], F32)
@@ -373,7 +385,8 @@ def tile_netvlad_k_kernel(tc, x, Wk, b, C, out):
             for f in range(FEATURE_TILES):
                 nc.tensor.transpose(out_psum[:, f, :], v_scaled[:, f * P : (f + 1) * P], identity[:])
             out_rows = work.tile([P, FEATURE_TILES, CLUSTERS], F32)
-            nc.scalar.copy(out=out_rows[:], in_=out_psum[:])
+            copy_out = (nc.scalar.copy, nc.vector.tensor_copy)[image]
+            copy_out(out=out_rows[:], in_=out_psum[:])
             nc.sync.dma_start(
                 out=out[image, :].rearrange("(f p k) -> p f k", f=FEATURE_TILES, p=P),
                 in_=out_rows[:],

@@ -27,6 +27,8 @@ FEATURE_TILES = FEATURES // P
 WORDS = FEATURES // 2
 
 POOL_FEATURES = 176
+VECTOR_FEATURES = 24
+SCALAR_FROM = POOL_FEATURES + VECTOR_FEATURES
 IN_BUFS = 3
 WIDTH = FEATURES * PACK
 
@@ -271,9 +273,13 @@ def tile_netvlad_k_kernel(tc, x, Wk, b, C, out):
 
         def group_positions(c):
             xn = quantise_input[c][:, WIDTH:].rearrange("p (d j) -> p d j", j=PACK)
+            nc.vector.tensor_copy(
+                out=xn[:, POOL_FEATURES:SCALAR_FROM, :].rearrange("p (g i) j -> p g j i", i=4),
+                in_=x_natural[c][:, :, POOL_FEATURES:SCALAR_FROM].rearrange("p j (g i) -> p g j i", i=4),
+            )
             nc.scalar.copy(
-                out=xn[:, POOL_FEATURES:, :].rearrange("p (g i) j -> p g j i", i=4),
-                in_=x_natural[c][:, :, POOL_FEATURES:].rearrange("p j (g i) -> p g j i", i=4),
+                out=xn[:, SCALAR_FROM:, :].rearrange("p (g i) j -> p g j i", i=4),
+                in_=x_natural[c][:, :, SCALAR_FROM:].rearrange("p j (g i) -> p g j i", i=4),
             )
 
         def second_matmul(c):

@@ -51,7 +51,7 @@ FIRST_STEP = -AT_TRANSPOSE
 LAST_EXP_STEP = CHUNKS - 1 - AT_EXP
 LAST_STEP = CHUNKS - 1 - AT_FINISH_IMAGE
 
-SUM_COLUMNS = 64
+SUM_COLUMNS = 96
 
 FLOPS = 2 * 2 * IMAGES * POSITIONS * FEATURES * CLUSTERS
 
@@ -91,23 +91,26 @@ def tile_netvlad_k_kernel(tc, x, Wk, b, C, out):
             image, chunk_in_image = divmod(c, CHUNKS_PER_IMAGE)
             first = chunk_in_image * CHUNK
             x_nat = x_pool.tile([P, PACK, FEATURES], BF16)
-            nc.sync.dma_start(
-                out=x_nat[:],
-                in_=x_rows[image, first : first + CHUNK, :].rearrange("(p j) d -> p j d", j=PACK),
-            )
+            in_rows = x_rows[image, first : first + CHUNK, :].rearrange("(p j) d -> p j d", j=PACK)
+            pieces = 2 if c == 0 else 1
+            for piece in range(pieces):
+                j_piece = slice(piece * PACK // pieces, (piece + 1) * PACK // pieces)
+                nc.sync.dma_start(out=x_nat[:, j_piece, :], in_=in_rows[:, j_piece, :])
             x_natural[c] = x_nat
 
-        for c in range(FIRST_STEP + AT_LOAD):
-            load(c)
-
+        load(0)
         identity = const.tile([P, P], F32)
         make_identity(nc, identity[:])
         ones = const.tile([P, P], F32)
         nc.vector.memset(ones[:], 1.0)
+        ones_bf16 = const.tile([P, P], BF16)
+        nc.vector.memset(ones_bf16[:], 1.0)
+        bias_row = const.tile([P, CLUSTERS], BF16)
+        nc.vector.memset(bias_row[:], 0.0)
 
         wk_raw = const.tile([P, PACK, CLUSTERS], BF16)
         for u in range(2):
-            nc.scalar.dma_start(
+            nc.sync.dma_start(
                 out=wk_raw[:, 2 * u : 2 * u + 2, :],
                 in_=Wk[u * 2 * P : (u + 1) * 2 * P, :].rearrange("(q e) k -> q e k", e=2),
             )
@@ -116,10 +119,15 @@ def tile_netvlad_k_kernel(tc, x, Wk, b, C, out):
         wk_codes = const.tile([P, CLUSTERS], U32, align_bytes=64)
         wk_scales = const.tile([P, CLUSTERS], U8, align_bytes=64)
 
-        bias_bf16 = const.tile([P, CLUSTERS], BF16)
-        nc.scalar.dma_start(out=bias_bf16[:], in_=b.partition_broadcast(P))
+        nc.sync.dma_start(out=bias_row[0:1, :], in_=b.unsqueeze(0))
         bias = const.tile([P, CLUSTERS], F32)
-        nc.vector.tensor_copy(out=bias[:], in_=bias_bf16[:])
+
+        def spread_bias():
+            bias_psum = s_psum.tile([P, CLUSTERS], F32, tag="s")
+            nc.tensor.matmul(
+                out=bias_psum[:], lhsT=ones_bf16[:], rhs=bias_row[:], start=True, stop=True
+            )
+            nc.vector.tensor_copy(out=bias[:], in_=bias_psum[:])
 
         nc.vector.quantize_mx(
             out=wk_codes[:].bitcast(FP8X4),
@@ -127,13 +135,16 @@ def tile_netvlad_k_kernel(tc, x, Wk, b, C, out):
             in_=wk_grouped[:].rearrange("q k t -> q (k t)"),
         )
 
+        for c in range(1, FIRST_STEP + AT_LOAD):
+            load(c)
+
         c_raw = const.tile([P, FEATURE_TILES, CLUSTERS], BF16)
-        nc.scalar.dma_start(out=c_raw[:], in_=C.rearrange("(f p) k -> p f k", p=P))
+        nc.sync.dma_start(out=c_raw[:], in_=C.rearrange("(f p) k -> p f k", p=P))
+        c_f32 = const.tile([P, FEATURE_TILES, CLUSTERS], F32)
+        nc.gpsimd.tensor_copy(out=c_f32[:], in_=c_raw[:])
         c_transposed = const.tile([P, FEATURES], F32)
 
         def transpose_centres():
-            c_f32 = const.tile([P, FEATURE_TILES, CLUSTERS], F32)
-            nc.vector.tensor_copy(out=c_f32[:], in_=c_raw[:])
             c_psum = s_psum.tile([P, FEATURE_TILES, P], F32, tag="s")
             for f in range(FEATURE_TILES):
                 nc.tensor.transpose(c_psum[:, f, :], c_f32[:, f, :], identity[:])
@@ -143,20 +154,17 @@ def tile_netvlad_k_kernel(tc, x, Wk, b, C, out):
         v_all = const.tile([P, IMAGES, FEATURES], F32)
         v_sumsq = const.tile([P, IMAGES], F32)
 
-        def transpose_features(c):
+        def transpose_features(c, h):
             x_words = x_natural[c][:].bitcast(F32)
-            banks = []
-            for h in range(2):
-                xt = xt_psum.tile([P, 2, 2 * P], F32, tag="xt")
-                for jj in range(2):
-                    for u in range(2):
-                        nc.tensor.transpose(
-                            xt[:, u, jj * P : (jj + 1) * P],
-                            x_words[:, 2 * h + jj, u * P : (u + 1) * P],
-                            identity[:],
-                        )
-                banks.append(xt)
-            x_transposed[c] = banks
+            xt = xt_psum.tile([P, 2, 2 * P], F32, tag="xt")
+            for jj in range(2):
+                for u in range(2):
+                    nc.tensor.transpose(
+                        xt[:, u, jj * P : (jj + 1) * P],
+                        x_words[:, 2 * h + jj, u * P : (u + 1) * P],
+                        identity[:],
+                    )
+            x_transposed[c, h] = xt
 
         def copy_transposed(c):
             xd = quantise_input[c - AT_QUANTISE][:, :WIDTH]
@@ -164,7 +172,7 @@ def tile_netvlad_k_kernel(tc, x, Wk, b, C, out):
             for h in range(2):
                 nc.scalar.copy(
                     out=xd_words[:, h * 2 * P : (h + 1) * 2 * P, :],
-                    in_=x_transposed[c][h][:].rearrange("q u n -> q n u"),
+                    in_=x_transposed[c, h][:].rearrange("q u n -> q n u"),
                 )
 
         def new_quantise_input(step):
@@ -333,15 +341,16 @@ def tile_netvlad_k_kernel(tc, x, Wk, b, C, out):
                 accum_out=v_sumsq[:, image : image + 1],
             )
 
-        def run(stage, c):
+        def run(stage, c, *rest):
             if 0 <= c < CHUNKS:
-                stage(c)
+                stage(c, *rest)
 
         def pipeline_step(step):
             run(load, step + AT_LOAD)
             run(add_centres, step + AT_FINISH_IMAGE)
-            run(transpose_features, step + AT_TRANSPOSE)
+            run(transpose_features, step + AT_TRANSPOSE, 0)
             run(second_matmul, step + AT_SECOND_MATMUL)
+            run(transpose_features, step + AT_TRANSPOSE, 1)
             run(first_matmul, step + AT_FIRST_MATMUL)
             run(exponentials, step + AT_EXP)
             run(copy_transposed, step + AT_COPY_TRANSPOSED)
@@ -358,7 +367,9 @@ def tile_netvlad_k_kernel(tc, x, Wk, b, C, out):
 
         for step in range(FIRST_STEP, FIRST_STEP + IN_BUFS):
             new_quantise_input(step)
-        for step in range(FIRST_STEP, 0):
+        pipeline_step(FIRST_STEP)
+        spread_bias()
+        for step in range(FIRST_STEP + 1, 0):
             pipeline_step(step)
         transpose_centres()
         for step in range(0, LAST_EXP_STEP + 1):
@@ -372,15 +383,26 @@ def tile_netvlad_k_kernel(tc, x, Wk, b, C, out):
         nc.vector.tensor_scalar_add(out=cluster_inv[:], in0=v_sumsq[:], scalar1=EPS)
         nc.vector.reciprocal(out=cluster_inv[:], in_=cluster_inv[:])
         cluster_unit = const.tile([P, IMAGES], F32)
-        nc.vector.tensor_tensor(out=cluster_unit[:], in0=v_sumsq[:], in1=cluster_inv[:], op=ALU.mult)
+        nc.vector.tensor_scalar(
+            out=cluster_unit[:],
+            in0=cluster_inv[:],
+            scalar1=-EPS,
+            scalar2=1.0 + EPS / CLUSTERS,
+            op0=ALU.mult,
+            op1=ALU.add,
+        )
         total_psum = s_psum.tile([P, IMAGES], F32, tag="s")
         nc.tensor.matmul(out=total_psum[:], lhsT=ones[:], rhs=cluster_unit[:], start=True, stop=True)
         image_inv = const.tile([P, IMAGES], F32)
-        nc.vector.tensor_scalar_add(out=image_inv[:], in0=total_psum[:], scalar1=EPS)
-        nc.vector.reciprocal(out=image_inv[:], in_=image_inv[:])
+        nc.vector.reciprocal(out=image_inv[:], in_=total_psum[:])
         factor = const.tile([P, IMAGES], F32)
-        nc.vector.tensor_tensor(out=factor[:], in0=cluster_inv[:], in1=image_inv[:], op=ALU.mult)
-        nc.scalar.sqrt(out=factor[:], in_=factor[:])
+        for image in range(IMAGES):
+            nc.scalar.activation(
+                out=factor[:, image : image + 1],
+                in_=cluster_inv[:, image : image + 1],
+                func=ACT.Sqrt,
+                scale=image_inv[:, image : image + 1],
+            )
 
         for image in range(IMAGES):
             v_scaled = work.tile([P, FEATURES], F32)

@@ -26,9 +26,7 @@ CHUNKS = IMAGES * CHUNKS_PER_IMAGE
 FEATURE_TILES = FEATURES // P
 WORDS = FEATURES // 2
 
-POOL_FEATURES = 176
-VECTOR_FEATURES = 24
-SCALAR_FROM = POOL_FEATURES + VECTOR_FEATURES
+POOL_FEATURES = 240
 IN_BUFS = 3
 WIDTH = FEATURES * PACK
 
@@ -66,7 +64,8 @@ def tile_netvlad_k_kernel(tc, x, Wk, b, C, out):
         work = ctx.enter_context(tc.tile_pool(name="work", bufs=4))
         in_pool = ctx.enter_context(tc.tile_pool(name="in_pool", bufs=IN_BUFS))
         held = ctx.enter_context(tc.tile_pool(name="held", bufs=5))
-        xt_psum = ctx.enter_context(tc.psum_pool(name="xt_psum", bufs=4))
+        xt_psum = ctx.enter_context(tc.psum_pool(name="xt_psum", bufs=3))
+        r_psum = ctx.enter_context(tc.psum_pool(name="r_psum", bufs=1))
         s_psum = ctx.enter_context(tc.psum_pool(name="s_psum", bufs=2))
         v_psum = ctx.enter_context(tc.psum_pool(name="v_psum", bufs=1))
         sum_psum = ctx.enter_context(tc.psum_pool(name="sum_psum", bufs=1))
@@ -82,6 +81,7 @@ def tile_netvlad_k_kernel(tc, x, Wk, b, C, out):
         exps = {}
         exp_sums = {}
         recip_sums = {}
+        recips_psum = {}
         a_grouped = {}
         a_quantised = {}
         xn_quantised = {}
@@ -248,12 +248,19 @@ def tile_netvlad_k_kernel(tc, x, Wk, b, C, out):
             nc.vector.reciprocal(out=e_recip[:], in_=exp_sums[c][:])
             recip_sums[c] = e_recip
 
+        def copy_recips(c):
+            r_bank = r_psum.tile([P, PACK], F32, tag="r")
+            nc.tensor.matmul(
+                out=r_bank[:], lhsT=identity[:], rhs=recip_sums[c][:], start=True, stop=True
+            )
+            recips_psum[c] = r_bank
+
         def normalise(c):
             a_words = work.tile([P, CLUSTERS, PACK], BF16, align_bytes=64)
             nc.vector.tensor_tensor(
                 out=a_words[:].rearrange("p (g i) j -> p g j i", i=4),
                 in0=exps[c][:].rearrange("p j (g i) -> p g j i", i=4),
-                in1=recip_sums[c][:].unsqueeze(1).unsqueeze(3).to_broadcast([P, CLUSTERS // 4, PACK, 4]),
+                in1=recips_psum[c][:].unsqueeze(1).unsqueeze(3).to_broadcast([P, CLUSTERS // 4, PACK, 4]),
                 op=ALU.mult,
             )
             a_grouped[c] = a_words
@@ -281,13 +288,9 @@ def tile_netvlad_k_kernel(tc, x, Wk, b, C, out):
 
         def group_positions(c):
             xn = quantise_input[c][:, WIDTH:].rearrange("p (d j) -> p d j", j=PACK)
-            nc.vector.tensor_copy(
-                out=xn[:, POOL_FEATURES:SCALAR_FROM, :].rearrange("p (g i) j -> p g j i", i=4),
-                in_=x_natural[c][:, :, POOL_FEATURES:SCALAR_FROM].rearrange("p j (g i) -> p g j i", i=4),
-            )
             nc.scalar.copy(
-                out=xn[:, SCALAR_FROM:, :].rearrange("p (g i) j -> p g j i", i=4),
-                in_=x_natural[c][:, :, SCALAR_FROM:].rearrange("p j (g i) -> p g j i", i=4),
+                out=xn[:, POOL_FEATURES:, :].rearrange("p (g i) j -> p g j i", i=4),
+                in_=x_natural[c][:, :, POOL_FEATURES:].rearrange("p j (g i) -> p g j i", i=4),
             )
 
         def second_matmul(c):
@@ -348,6 +351,7 @@ def tile_netvlad_k_kernel(tc, x, Wk, b, C, out):
         def pipeline_step(step):
             run(load, step + AT_LOAD)
             run(add_centres, step + AT_FINISH_IMAGE)
+            run(copy_recips, step + AT_NORMALISE)
             run(transpose_features, step + AT_TRANSPOSE, 0)
             run(second_matmul, step + AT_SECOND_MATMUL)
             run(transpose_features, step + AT_TRANSPOSE, 1)
@@ -356,8 +360,8 @@ def tile_netvlad_k_kernel(tc, x, Wk, b, C, out):
             run(copy_transposed, step + AT_COPY_TRANSPOSED)
             run(add_bias, step + AT_BIAS)
             run(row_max, step + AT_MAX)
-            run(invert_sums, step + AT_INVERT_SUMS)
             run(normalise, step + AT_NORMALISE)
+            run(invert_sums, step + AT_INVERT_SUMS)
             run(group_positions, step + AT_GROUP_POSITIONS)
             run(sum_squares, step + AT_FINISH_IMAGE)
             quantise(step)

@@ -26,7 +26,7 @@ CHUNKS = IMAGES * CHUNKS_PER_IMAGE
 FEATURE_TILES = FEATURES // P
 WORDS = FEATURES // 2
 
-POOL_FEATURES = 240
+POOL_FEATURES = 256
 IN_BUFS = 3
 WIDTH = FEATURES * PACK
 
@@ -43,11 +43,17 @@ AT_INVERT_SUMS = 0
 AT_NORMALISE = -1
 AT_POOL_GROUP_POSITIONS = IN_BUFS
 AT_QUANTISE_ASSIGNMENTS = -1
+AT_SUM = -1
+AT_SAVE_SUM = -2
 AT_SECOND_MATMUL = -2
 AT_FINISH_IMAGE = -3
+AT_ADD_EPS = -4
+AT_INVERT_SUMSQ = -5
+AT_CLUSTER_UNIT = -6
 FIRST_STEP = -AT_TRANSPOSE
 LAST_EXP_STEP = CHUNKS - 1 - AT_EXP
-LAST_STEP = CHUNKS - 1 - AT_FINISH_IMAGE
+LAST_MATMUL_STEP = CHUNKS - 1 - AT_SECOND_MATMUL
+LAST_STEP = CHUNKS - 1 - AT_CLUSTER_UNIT
 
 SUM_COLUMNS = 96
 
@@ -148,9 +154,10 @@ def tile_netvlad_k_kernel(tc, x, Wk, b, C, out):
             c_psum = s_psum.tile([P, FEATURE_TILES, P], F32, tag="s")
             for f in range(FEATURE_TILES):
                 nc.tensor.transpose(c_psum[:, f, :], c_f32[:, f, :], identity[:])
-            nc.vector.tensor_copy(out=c_transposed[:], in_=c_psum[:].rearrange("k f p -> k (f p)"))
+            nc.scalar.copy(out=c_transposed[:], in_=c_psum[:].rearrange("k f p -> k (f p)"))
 
         a_sums_psum = sum_psum.tile([P, IMAGES, SUM_COLUMNS], F32, tag="sums")
+        a_sums = const.tile([P, IMAGES], F32)
         v_all = const.tile([P, IMAGES, FEATURES], F32)
         v_sumsq = const.tile([P, IMAGES], F32)
 
@@ -293,7 +300,7 @@ def tile_netvlad_k_kernel(tc, x, Wk, b, C, out):
                 in_=x_natural[c][:, :, POOL_FEATURES:].rearrange("p j (g i) -> p g j i", i=4),
             )
 
-        def second_matmul(c):
+        def sum_assignments(c):
             image, chunk_in_image = divmod(c, CHUNKS_PER_IMAGE)
             first = chunk_in_image == 0
             last = chunk_in_image == CHUNKS_PER_IMAGE - 1
@@ -305,6 +312,16 @@ def tile_netvlad_k_kernel(tc, x, Wk, b, C, out):
                     start=first and j == 0,
                     stop=last and j == PACK - 1,
                 )
+
+        def save_sum(c):
+            image, chunk_in_image = divmod(c, CHUNKS_PER_IMAGE)
+            if chunk_in_image == CHUNKS_PER_IMAGE - 1:
+                nc.vector.tensor_copy(out=a_sums[:, image : image + 1], in_=a_sums_psum[:, image, 0:1])
+
+        def second_matmul(c):
+            image, chunk_in_image = divmod(c, CHUNKS_PER_IMAGE)
+            first = chunk_in_image == 0
+            last = chunk_in_image == CHUNKS_PER_IMAGE - 1
             if first:
                 v_bank = v_psum.tile([P, FEATURES], F32, tag="v")
                 v_banks[image] = v_bank
@@ -326,7 +343,7 @@ def tile_netvlad_k_kernel(tc, x, Wk, b, C, out):
                 nc.vector.scalar_tensor_tensor(
                     out=v_all[:, image, :],
                     in0=c_transposed[:],
-                    scalar=a_sums_psum[:, image, 0:1],
+                    scalar=a_sums[:, image : image + 1],
                     in1=v_banks[image][:],
                     op0=ALU.mult,
                     op1=ALU.add,
@@ -344,6 +361,36 @@ def tile_netvlad_k_kernel(tc, x, Wk, b, C, out):
                 accum_out=v_sumsq[:, image : image + 1],
             )
 
+        cluster_inv = const.tile([P, IMAGES], F32)
+        cluster_unit = const.tile([P, IMAGES], F32)
+        image_inv = const.tile([P, IMAGES], F32)
+        factor = const.tile([P, IMAGES], F32)
+
+        def add_eps(c):
+            image, chunk_in_image = divmod(c, CHUNKS_PER_IMAGE)
+            if chunk_in_image == CHUNKS_PER_IMAGE - 1:
+                col = slice(image, image + 1)
+                nc.vector.tensor_scalar_add(out=cluster_inv[:, col], in0=v_sumsq[:, col], scalar1=EPS)
+
+        def invert_sumsq(c):
+            image, chunk_in_image = divmod(c, CHUNKS_PER_IMAGE)
+            if chunk_in_image == CHUNKS_PER_IMAGE - 1:
+                col = slice(image, image + 1)
+                nc.vector.reciprocal(out=cluster_inv[:, col], in_=cluster_inv[:, col])
+
+        def sum_of_unit_cluster(c):
+            image, chunk_in_image = divmod(c, CHUNKS_PER_IMAGE)
+            if chunk_in_image == CHUNKS_PER_IMAGE - 1:
+                col = slice(image, image + 1)
+                nc.vector.tensor_scalar(
+                    out=cluster_unit[:, col],
+                    in0=cluster_inv[:, col],
+                    scalar1=-EPS,
+                    scalar2=1.0 + EPS / CLUSTERS,
+                    op0=ALU.mult,
+                    op1=ALU.add,
+                )
+
         def run(stage, c, *rest):
             if 0 <= c < CHUNKS:
                 stage(c, *rest)
@@ -351,8 +398,10 @@ def tile_netvlad_k_kernel(tc, x, Wk, b, C, out):
         def pipeline_step(step):
             run(load, step + AT_LOAD)
             run(add_centres, step + AT_FINISH_IMAGE)
+            run(save_sum, step + AT_SAVE_SUM)
             run(copy_recips, step + AT_NORMALISE)
             run(transpose_features, step + AT_TRANSPOSE, 0)
+            run(sum_assignments, step + AT_SUM)
             run(second_matmul, step + AT_SECOND_MATMUL)
             run(transpose_features, step + AT_TRANSPOSE, 1)
             run(first_matmul, step + AT_FIRST_MATMUL)
@@ -364,6 +413,9 @@ def tile_netvlad_k_kernel(tc, x, Wk, b, C, out):
             run(invert_sums, step + AT_INVERT_SUMS)
             run(group_positions, step + AT_GROUP_POSITIONS)
             run(sum_squares, step + AT_FINISH_IMAGE)
+            run(add_eps, step + AT_ADD_EPS)
+            run(invert_sumsq, step + AT_INVERT_SUMSQ)
+            run(sum_of_unit_cluster, step + AT_CLUSTER_UNIT)
             quantise(step)
             run(quantise_assignments, step + AT_QUANTISE_ASSIGNMENTS)
             new_quantise_input(step + IN_BUFS)
@@ -376,50 +428,54 @@ def tile_netvlad_k_kernel(tc, x, Wk, b, C, out):
         for step in range(FIRST_STEP + 1, 0):
             pipeline_step(step)
         transpose_centres()
-        for step in range(0, LAST_EXP_STEP + 1):
-            pipeline_step(step)
-        unit = const.tile([P, 1], F32)
-        nc.scalar.sqrt(out=unit[:], in_=ones[:, 0:1])
-        for step in range(LAST_EXP_STEP + 1, LAST_STEP + 1):
-            pipeline_step(step)
+        def add_up_clusters(image):
+            col = slice(image, image + 1)
+            total_psum = s_psum.tile([P, 1], F32, tag="s")
+            nc.tensor.matmul(
+                out=total_psum[:], lhsT=ones[:], rhs=cluster_unit[:, col], start=True, stop=True
+            )
+            return total_psum
 
-        cluster_inv = const.tile([P, IMAGES], F32)
-        nc.vector.tensor_scalar_add(out=cluster_inv[:], in0=v_sumsq[:], scalar1=EPS)
-        nc.vector.reciprocal(out=cluster_inv[:], in_=cluster_inv[:])
-        cluster_unit = const.tile([P, IMAGES], F32)
-        nc.vector.tensor_scalar(
-            out=cluster_unit[:],
-            in0=cluster_inv[:],
-            scalar1=-EPS,
-            scalar2=1.0 + EPS / CLUSTERS,
-            op0=ALU.mult,
-            op1=ALU.add,
-        )
-        total_psum = s_psum.tile([P, IMAGES], F32, tag="s")
-        nc.tensor.matmul(out=total_psum[:], lhsT=ones[:], rhs=cluster_unit[:], start=True, stop=True)
-        image_inv = const.tile([P, IMAGES], F32)
-        nc.vector.reciprocal(out=image_inv[:], in_=total_psum[:])
-        factor = const.tile([P, IMAGES], F32)
-        for image in range(IMAGES):
+        def scale_on_vector(out, in_, by):
+            nc.vector.tensor_scalar_mul(out=out, in0=in_, scalar1=by)
+
+        def scale_on_scalar(out, in_, by):
+            nc.scalar.activation(out=out, in_=in_, func=ACT.Copy, scale=by)
+
+        def scale_image(image, total_psum, scales):
+            col = slice(image, image + 1)
+            nc.vector.reciprocal(out=image_inv[:, col], in_=total_psum[:])
             nc.scalar.activation(
-                out=factor[:, image : image + 1],
-                in_=cluster_inv[:, image : image + 1],
-                func=ACT.Sqrt,
-                scale=image_inv[:, image : image + 1],
+                out=factor[:, col], in_=cluster_inv[:, col], func=ACT.Sqrt, scale=image_inv[:, col]
             )
+            for h in range(2):
+                v_scaled = work.tile([P, half * P], F32)
+                scales[h](v_scaled[:], v_all[:, image, h * half * P : (h + 1) * half * P], factor[:, col])
+                scaled_halves[image, h] = v_scaled
 
-        for image in range(IMAGES):
-            v_scaled = work.tile([P, FEATURES], F32)
-            nc.vector.tensor_scalar_mul(
-                out=v_scaled[:], in0=v_all[:, image, :], scalar1=factor[:, image : image + 1]
-            )
-            out_psum = xt_psum.tile([P, FEATURE_TILES, CLUSTERS], F32, tag="xt")
-            for f in range(FEATURE_TILES):
-                nc.tensor.transpose(out_psum[:, f, :], v_scaled[:, f * P : (f + 1) * P], identity[:])
-            out_rows = work.tile([P, FEATURE_TILES, CLUSTERS], F32)
-            copy_out = (nc.scalar.copy, nc.vector.tensor_copy)[image]
-            copy_out(out=out_rows[:], in_=out_psum[:])
-            nc.sync.dma_start(
-                out=out[image, :].rearrange("(f p k) -> p f k", f=FEATURE_TILES, p=P),
-                in_=out_rows[:],
-            )
+        def store(image, copies):
+            out_tiles = out[image, :].rearrange("(f p k) -> p f k", f=FEATURE_TILES, p=P)
+            for h in range(2):
+                v_scaled = scaled_halves[image, h]
+                out_psum = xt_psum.tile([P, half, CLUSTERS], F32, tag="xt")
+                for f in range(half):
+                    nc.tensor.transpose(out_psum[:, f, :], v_scaled[:, f * P : (f + 1) * P], identity[:])
+                out_rows = work.tile([P, half, CLUSTERS], F32)
+                copies[h](out=out_rows[:], in_=out_psum[:])
+                nc.sync.dma_start(out=out_tiles[:, h * half : (h + 1) * half, :], in_=out_rows[:])
+
+        half = FEATURE_TILES // 2
+        scaled_halves = {}
+
+        for step in range(0, LAST_EXP_STEP):
+            pipeline_step(step)
+        first_total = add_up_clusters(0)
+        pipeline_step(LAST_EXP_STEP)
+        scale_image(0, first_total, (scale_on_scalar, scale_on_scalar))
+        for step in range(LAST_EXP_STEP + 1, LAST_MATMUL_STEP + 1):
+            pipeline_step(step)
+        store(0, (nc.scalar.copy, nc.scalar.copy))
+        for step in range(LAST_MATMUL_STEP + 1, LAST_STEP + 1):
+            pipeline_step(step)
+        scale_image(1, add_up_clusters(1), (scale_on_vector, scale_on_scalar))
+        store(1, (nc.vector.tensor_copy, nc.scalar.copy))

from contextlib import ExitStack

import concourse.mybir as mybir
from concourse.masks import make_identity

F32 = mybir.dt.float32
BF16 = mybir.dt.bfloat16
U32 = mybir.dt.uint32
U8 = mybir.dt.uint8
FP8X4 = mybir.dt.float8_e4m3fn_x4
ALU = mybir.AluOpType
ACT = mybir.ActivationFunctionType
AXIS = mybir.AxisListType

P = 128
PACK = 4
IMAGES = 2
POSITIONS = 16384
FEATURES = 512
CLUSTERS = 128
EPS = 1e-12

CHUNK = P * PACK
CHUNKS_PER_IMAGE = POSITIONS // CHUNK
CHUNKS = IMAGES * CHUNKS_PER_IMAGE
FEATURE_TILES = FEATURES // P
WORDS = FEATURES // 2

POOL_FEATURES = 256
IN_BUFS = 3
WIDTH = FEATURES * PACK

AT_LOAD = 11
AT_TRANSPOSE = 7
AT_COPY_TRANSPOSED = 6
AT_QUANTISE = 5
AT_FIRST_MATMUL = 4
AT_BIAS = 3
AT_MAX = 2
AT_EXP = 1
AT_GROUP_POSITIONS = 1
AT_INVERT_SUMS = 0
AT_NORMALISE = -1
AT_POOL_GROUP_POSITIONS = IN_BUFS
AT_QUANTISE_ASSIGNMENTS = -1
AT_SUM = -1
AT_SAVE_SUM = -2
AT_SECOND_MATMUL = -2
AT_FINISH_IMAGE = -3
AT_ADD_EPS = -4
AT_INVERT_SUMSQ = -5
AT_CLUSTER_UNIT = -6
FIRST_STEP = -AT_TRANSPOSE
LAST_EXP_STEP = CHUNKS - 1 - AT_EXP
LAST_MATMUL_STEP = CHUNKS - 1 - AT_SECOND_MATMUL
LAST_STEP = CHUNKS - 1 - AT_CLUSTER_UNIT

SUM_COLUMNS = 96

FLOPS = 2 * 2 * IMAGES * POSITIONS * FEATURES * CLUSTERS


def tile_netvlad_k_kernel(tc, x, Wk, b, C, out):
    nc = tc.nc
    x_rows = x.rearrange("i h w d -> i (h w) d")

    with ExitStack() as ctx:
        const = ctx.enter_context(tc.tile_pool(name="const", bufs=1))
        x_pool = ctx.enter_context(tc.tile_pool(name="x_pool", bufs=AT_LOAD - AT_GROUP_POSITIONS + 2))
        work = ctx.enter_context(tc.tile_pool(name="work", bufs=4))
        in_pool = ctx.enter_context(tc.tile_pool(name="in_pool", bufs=IN_BUFS))
        held = ctx.enter_context(tc.tile_pool(name="held", bufs=5))
        xt_psum = ctx.enter_context(tc.psum_pool(name="xt_psum", bufs=3))
        r_psum = ctx.enter_context(tc.psum_pool(name="r_psum", bufs=1))
        s_psum = ctx.enter_context(tc.psum_pool(name="s_psum", bufs=2))
        v_psum = ctx.enter_context(tc.psum_pool(name="v_psum", bufs=1))
        sum_psum = ctx.enter_context(tc.psum_pool(name="sum_psum", bufs=1))
        ctx.enter_context(tc.manual_schedule())

        x_natural = {}
        x_transposed = {}
        quantise_input = {}
        xd_quantised = {}
        logits_psum = {}
        logits = {}
        neg_max = {}
        exps = {}
        exp_sums = {}
        recip_sums = {}
        recips_psum = {}
        a_grouped = {}
        a_quantised = {}
        xn_quantised = {}
        v_banks = {}

        def load(c):
            image, chunk_in_image = divmod(c, CHUNKS_PER_IMAGE)
            first = chunk_in_image * CHUNK
            x_nat = x_pool.tile([P, PACK, FEATURES], BF16)
            in_rows = x_rows[image, first : first + CHUNK, :].rearrange("(p j) d -> p j d", j=PACK)
            pieces = 2 if c == 0 else 1
            for piece in range(pieces):
                j_piece = slice(piece * PACK // pieces, (piece + 1) * PACK // pieces)
                nc.sync.dma_start(out=x_nat[:, j_piece, :], in_=in_rows[:, j_piece, :])
            x_natural[c] = x_nat

        load(0)
        identity = const.tile([P, P], F32)
        make_identity(nc, identity[:])
        ones = const.tile([P, P], F32)
        nc.vector.memset(ones[:], 1.0)
        ones_bf16 = const.tile([P, P], BF16)
        nc.vector.memset(ones_bf16[:], 1.0)
        bias_row = const.tile([P, CLUSTERS], BF16)
        nc.vector.memset(bias_row[:], 0.0)

        wk_raw = const.tile([P, PACK, CLUSTERS], BF16)
        for u in range(2):
            nc.sync.dma_start(
                out=wk_raw[:, 2 * u : 2 * u + 2, :],
                in_=Wk[u * 2 * P : (u + 1) * 2 * P, :].rearrange("(q e) k -> q e k", e=2),
            )
        wk_grouped = const.tile([P, CLUSTERS, PACK], BF16, align_bytes=64)
        nc.vector.tensor_copy(out=wk_grouped[:], in_=wk_raw[:].rearrange("q t k -> q k t"))
        wk_codes = const.tile([P, CLUSTERS], U32, align_bytes=64)
        wk_scales = const.tile([P, CLUSTERS], U8, align_bytes=64)

        nc.sync.dma_start(out=bias_row[0:1, :], in_=b.unsqueeze(0))
        bias = const.tile([P, CLUSTERS], F32)

        def spread_bias():
            bias_psum = s_psum.tile([P, CLUSTERS], F32, tag="s")
            nc.tensor.matmul(
                out=bias_psum[:], lhsT=ones_bf16[:], rhs=bias_row[:], start=True, stop=True
            )
            nc.vector.tensor_copy(out=bias[:], in_=bias_psum[:])

        nc.vector.quantize_mx(
            out=wk_codes[:].bitcast(FP8X4),
            scales=wk_scales[:],
            in_=wk_grouped[:].rearrange("q k t -> q (k t)"),
        )

        for c in range(1, FIRST_STEP + AT_LOAD):
            load(c)

        c_raw = const.tile([P, FEATURE_TILES, CLUSTERS], BF16)
        nc.sync.dma_start(out=c_raw[:], in_=C.rearrange("(f p) k -> p f k", p=P))
        c_f32 = const.tile([P, FEATURE_TILES, CLUSTERS], F32)
        nc.gpsimd.tensor_copy(out=c_f32[:], in_=c_raw[:])
        c_transposed = const.tile([P, FEATURES], F32)

        def transpose_centres():
            c_psum = s_psum.tile([P, FEATURE_TILES, P], F32, tag="s")
            for f in range(FEATURE_TILES):
                nc.tensor.transpose(c_psum[:, f, :], c_f32[:, f, :], identity[:])
            nc.scalar.copy(out=c_transposed[:], in_=c_psum[:].rearrange("k f p -> k (f p)"))

        a_sums_psum = sum_psum.tile([P, IMAGES, SUM_COLUMNS], F32, tag="sums")
        a_sums = const.tile([P, IMAGES], F32)
        v_all = const.tile([P, IMAGES, FEATURES], F32)
        v_sumsq = const.tile([P, IMAGES], F32)

        def transpose_features(c, h):
            x_words = x_natural[c][:].bitcast(F32)
            xt = xt_psum.tile([P, 2, 2 * P], F32, tag="xt")
            for jj in range(2):
                for u in range(2):
                    nc.tensor.transpose(
                        xt[:, u, jj * P : (jj + 1) * P],
                        x_words[:, 2 * h + jj, u * P : (u + 1) * P],
                        identity[:],
                    )
            x_transposed[c, h] = xt

        def copy_transposed(c):
            xd = quantise_input[c - AT_QUANTISE][:, :WIDTH]
            xd_words = xd.bitcast(F32).rearrange("q (n u) -> q n u", u=2)
            for h in range(2):
                nc.scalar.copy(
                    out=xd_words[:, h * 2 * P : (h + 1) * 2 * P, :],
                    in_=x_transposed[c, h][:].rearrange("q u n -> q n u"),
                )

        def new_quantise_input(step):
            q_in = in_pool.tile([P, 2 * WIDTH], BF16, align_bytes=64)
            quantise_input[step] = q_in

        def quantise(step):
            along_d = 0 <= step + AT_QUANTISE < CHUNKS
            along_n = 0 <= step < CHUNKS
            if not along_d and not along_n:
                return
            first = 0 if along_d else 1
            last = 2 if along_n else 1
            codes = held.tile([P, 2 * CHUNK], U32, align_bytes=64)
            scales = held.tile([P, 2 * CHUNK], U8, align_bytes=64)
            nc.vector.quantize_mx(
                out=codes[:, first * CHUNK : last * CHUNK].bitcast(FP8X4),
                scales=scales[:, first * CHUNK : last * CHUNK],
                in_=quantise_input[step][:, first * WIDTH : last * WIDTH],
            )
            xd_quantised[step + AT_QUANTISE] = (codes[:, :CHUNK], scales[:, :CHUNK])
            xn_quantised[step] = (codes[:, CHUNK:], scales[:, CHUNK:])

        def first_matmul(c):
            xd_codes, xd_scales = xd_quantised[c]
            s_bank = s_psum.tile([P, PACK, CLUSTERS], F32, tag="s")
            for j in range(PACK):
                nc.tensor.matmul_mx(
                    out=s_bank[:, j, :],
                    lhsT=xd_codes[:, j * P : (j + 1) * P].bitcast(FP8X4),
                    lhsT_scale=xd_scales[:, j * P : (j + 1) * P],
                    rhs=wk_codes[:].bitcast(FP8X4),
                    rhs_scale=wk_scales[:],
                    start=True,
                    stop=True,
                )
            logits_psum[c] = s_bank

        def add_bias(c):
            s_biased = work.tile([P, PACK, CLUSTERS], F32)
            nc.vector.tensor_tensor(
                out=s_biased[:],
                in0=logits_psum[c][:],
                in1=bias[:].unsqueeze(1).to_broadcast([P, PACK, CLUSTERS]),
                op=ALU.add,
            )
            logits[c] = s_biased

        def row_max(c):
            minus_max = work.tile([P, PACK], F32)
            nc.vector.tensor_reduce(
                out=minus_max[:], in_=logits[c][:], axis=AXIS.X, op=ALU.max, negate=True
            )
            neg_max[c] = minus_max

        def exponentials(c):
            e = held.tile([P, PACK, CLUSTERS], F32)
            e_sum = work.tile([P, PACK], F32)
            for j in range(PACK):
                nc.scalar.activation(
                    out=e[:, j, :],
                    in_=logits[c][:, j, :],
                    func=ACT.Exp,
                    bias=neg_max[c][:, j : j + 1],
                    scale=1.0,
                    accum_out=e_sum[:, j : j + 1],
                )
            exps[c] = e
            exp_sums[c] = e_sum

        def invert_sums(c):
            e_recip = held.tile([P, PACK], F32)
            nc.vector.reciprocal(out=e_recip[:], in_=exp_sums[c][:])
            recip_sums[c] = e_recip

        def copy_recips(c):
            r_bank = r_psum.tile([P, PACK], F32, tag="r")
            nc.tensor.matmul(
                out=r_bank[:], lhsT=identity[:], rhs=recip_sums[c][:], start=True, stop=True
            )
            recips_psum[c] = r_bank

        def normalise(c):
            a_words = work.tile([P, CLUSTERS, PACK], BF16, align_bytes=64)
            nc.vector.tensor_tensor(
                out=a_words[:].rearrange("p (g i) j -> p g j i", i=4),
                in0=exps[c][:].rearrange("p j (g i) -> p g j i", i=4),
                in1=recips_psum[c][:].unsqueeze(1).unsqueeze(3).to_broadcast([P, CLUSTERS // 4, PACK, 4]),
                op=ALU.mult,
            )
            a_grouped[c] = a_words

        def quantise_assignments(c):
            a_codes = work.tile([P, CLUSTERS], U32, align_bytes=64)
            a_scales = work.tile([P, CLUSTERS], U8, align_bytes=64)
            nc.vector.quantize_mx(
                out=a_codes[:].bitcast(FP8X4),
                scales=a_scales[:],
                in_=a_grouped[c][:].rearrange("p k j -> p (k j)"),
            )
            a_quantised[c] = (a_codes, a_scales)

        def pool_group_positions(c):
            xn = quantise_input[c][:, WIDTH:].rearrange("p (d j) -> p d j", j=PACK)
            nc.gpsimd.tensor_scalar(
                out=xn[:, :POOL_FEATURES, :],
                in0=x_natural[c][:, :, :POOL_FEATURES].rearrange("p j d -> p d j"),
                scalar1=1.0,
                scalar2=0.0,
                op0=ALU.mult,
                op1=ALU.add,
            )

        def group_positions(c):
            xn = quantise_input[c][:, WIDTH:].rearrange("p (d j) -> p d j", j=PACK)
            nc.scalar.copy(
                out=xn[:, POOL_FEATURES:, :].rearrange("p (g i) j -> p g j i", i=4),
                in_=x_natural[c][:, :, POOL_FEATURES:].rearrange("p j (g i) -> p g j i", i=4),
            )

        def sum_assignments(c):
            image, chunk_in_image = divmod(c, CHUNKS_PER_IMAGE)
            first = chunk_in_image == 0
            last = chunk_in_image == CHUNKS_PER_IMAGE - 1
            for j in range(PACK):
                nc.tensor.matmul(
                    out=a_sums_psum[:, image, :],
                    lhsT=exps[c][:, j, :],
                    rhs=recip_sums[c][:, j : j + 1].to_broadcast([P, SUM_COLUMNS]),
                    start=first and j == 0,
                    stop=last and j == PACK - 1,
                )

        def save_sum(c):
            image, chunk_in_image = divmod(c, CHUNKS_PER_IMAGE)
            if chunk_in_image == CHUNKS_PER_IMAGE - 1:
                nc.vector.tensor_copy(out=a_sums[:, image : image + 1], in_=a_sums_psum[:, image, 0:1])

        def second_matmul(c):
            image, chunk_in_image = divmod(c, CHUNKS_PER_IMAGE)
            first = chunk_in_image == 0
            last = chunk_in_image == CHUNKS_PER_IMAGE - 1
            if first:
                v_bank = v_psum.tile([P, FEATURES], F32, tag="v")
                v_banks[image] = v_bank
            a_codes, a_scales = a_quantised[c]
            xn_codes, xn_scales = xn_quantised[c]
            nc.tensor.matmul_mx(
                out=v_banks[image][:],
                lhsT=a_codes[:].bitcast(FP8X4),
                lhsT_scale=a_scales[:],
                rhs=xn_codes.bitcast(FP8X4),
                rhs_scale=xn_scales,
                start=first,
                stop=last,
            )

        def add_centres(c):
            image, chunk_in_image = divmod(c, CHUNKS_PER_IMAGE)
            if chunk_in_image == CHUNKS_PER_IMAGE - 1:
                nc.vector.scalar_tensor_tensor(
                    out=v_all[:, image, :],
                    in0=c_transposed[:],
                    scalar=a_sums[:, image : image + 1],
                    in1=v_banks[image][:],
                    op0=ALU.mult,
                    op1=ALU.add,
                )

        def sum_squares(c):
            image, chunk_in_image = divmod(c, CHUNKS_PER_IMAGE)
            if chunk_in_image < CHUNKS_PER_IMAGE - 1:
                return
            squares = work.tile([P, FEATURES], F32)
            nc.scalar.activation(
                out=squares[:],
                in_=v_all[:, image, :],
                func=ACT.Square,
                accum_out=v_sumsq[:, image : image + 1],
            )

        cluster_inv = const.tile([P, IMAGES], F32)
        cluster_unit = const.tile([P, IMAGES], F32)
        image_inv = const.tile([P, IMAGES], F32)
        factor = const.tile([P, IMAGES], F32)

        def add_eps(c):
            image, chunk_in_image = divmod(c, CHUNKS_PER_IMAGE)
            if chunk_in_image == CHUNKS_PER_IMAGE - 1:
                col = slice(image, image + 1)
                nc.vector.tensor_scalar_add(out=cluster_inv[:, col], in0=v_sumsq[:, col], scalar1=EPS)

        def invert_sumsq(c):
            image, chunk_in_image = divmod(c, CHUNKS_PER_IMAGE)
            if chunk_in_image == CHUNKS_PER_IMAGE - 1:
                col = slice(image, image + 1)
                nc.vector.reciprocal(out=cluster_inv[:, col], in_=cluster_inv[:, col])

        def sum_of_unit_cluster(c):
            image, chunk_in_image = divmod(c, CHUNKS_PER_IMAGE)
            if chunk_in_image == CHUNKS_PER_IMAGE - 1:
                col = slice(image, image + 1)
                nc.vector.tensor_scalar(
                    out=cluster_unit[:, col],
                    in0=cluster_inv[:, col],
                    scalar1=-EPS,
                    scalar2=1.0 + EPS / CLUSTERS,
                    op0=ALU.mult,
                    op1=ALU.add,
                )

        def run(stage, c, *rest):
            if 0 <= c < CHUNKS:
                stage(c, *rest)

        def pipeline_step(step):
            run(load, step + AT_LOAD)
            run(add_centres, step + AT_FINISH_IMAGE)
            run(save_sum, step + AT_SAVE_SUM)
            run(copy_recips, step + AT_NORMALISE)
            run(transpose_features, step + AT_TRANSPOSE, 0)
            run(sum_assignments, step + AT_SUM)
            run(second_matmul, step + AT_SECOND_MATMUL)
            run(transpose_features, step + AT_TRANSPOSE, 1)
            run(first_matmul, step + AT_FIRST_MATMUL)
            run(exponentials, step + AT_EXP)
            run(copy_transposed, step + AT_COPY_TRANSPOSED)
            run(add_bias, step + AT_BIAS)
            run(row_max, step + AT_MAX)
            run(normalise, step + AT_NORMALISE)
            run(invert_sums, step + AT_INVERT_SUMS)
            run(group_positions, step + AT_GROUP_POSITIONS)
            run(sum_squares, step + AT_FINISH_IMAGE)
            run(add_eps, step + AT_ADD_EPS)
            run(invert_sumsq, step + AT_INVERT_SUMSQ)
            run(sum_of_unit_cluster, step + AT_CLUSTER_UNIT)
            quantise(step)
            run(quantise_assignments, step + AT_QUANTISE_ASSIGNMENTS)
            new_quantise_input(step + IN_BUFS)
            run(pool_group_positions, step + AT_POOL_GROUP_POSITIONS)

        for step in range(FIRST_STEP, FIRST_STEP + IN_BUFS):
            new_quantise_input(step)
        pipeline_step(FIRST_STEP)
        spread_bias()
        for step in range(FIRST_STEP + 1, 0):
            pipeline_step(step)
        transpose_centres()
        def add_up_clusters(image):
            col = slice(image, image + 1)
            total_psum = s_psum.tile([P, 1], F32, tag="s")
            nc.tensor.matmul(
                out=total_psum[:], lhsT=ones[:], rhs=cluster_unit[:, col], start=True, stop=True
            )
            return total_psum

        def scale_on_vector(out, in_, by):
            nc.vector.tensor_scalar_mul(out=out, in0=in_, scalar1=by)

        def scale_on_scalar(out, in_, by):
            nc.scalar.activation(out=out, in_=in_, func=ACT.Copy, scale=by)

        def scale_image(image, total_psum, scales):
            col = slice(image, image + 1)
            nc.vector.reciprocal(out=image_inv[:, col], in_=total_psum[:])
            nc.scalar.activation(
                out=factor[:, col], in_=cluster_inv[:, col], func=ACT.Sqrt, scale=image_inv[:, col]
            )
            for h in range(2):
                v_scaled = work.tile([P, half * P], F32)
                scales[h](v_scaled[:], v_all[:, image, h * half * P : (h + 1) * half * P], factor[:, col])
                scaled_halves[image, h] = v_scaled

        def store(image, copies):
            out_tiles = out[image, :].rearrange("(f p k) -> p f k", f=FEATURE_TILES, p=P)
            for h in range(2):
                v_scaled = scaled_halves[image, h]
                out_psum = xt_psum.tile([P, half, CLUSTERS], F32, tag="xt")
                for f in range(half):
                    nc.tensor.transpose(out_psum[:, f, :], v_scaled[:, f * P : (f + 1) * P], identity[:])
                out_rows = work.tile([P, half, CLUSTERS], F32)
                copies[h](out=out_rows[:], in_=out_psum[:])
                nc.sync.dma_start(out=out_tiles[:, h * half : (h + 1) * half, :], in_=out_rows[:])

        half = FEATURE_TILES // 2
        scaled_halves = {}

        for step in range(0, LAST_EXP_STEP):
            pipeline_step(step)
        first_total = add_up_clusters(0)
        pipeline_step(LAST_EXP_STEP)
        scale_image(0, first_total, (scale_on_scalar, scale_on_scalar))
        for step in range(LAST_EXP_STEP + 1, LAST_MATMUL_STEP + 1):
            pipeline_step(step)
        store(0, (nc.scalar.copy, nc.scalar.copy))
        for step in range(LAST_MATMUL_STEP + 1, LAST_STEP + 1):
            pipeline_step(step)
        scale_image(1, add_up_clusters(1), (scale_on_vector, scale_on_scalar))
        store(1, (nc.vector.tensor_copy, nc.scalar.copy))
